import numpy as np
import ml_dtypes


def mxq(x, axis, fmt="e4m3"):
    dtype, down = {"e4m3": (ml_dtypes.float8_e4m3fn, 7), "e5m2": (ml_dtypes.float8_e5m2, 14)}[fmt]
    v = np.moveaxis(np.asarray(x, np.float32).astype(ml_dtypes.bfloat16).astype(np.float64), axis, -1)
    blocks = v.reshape(v.shape[:-1] + (-1, 32))
    amax = np.abs(blocks).max(-1, keepdims=True)
    byte = np.maximum(np.where(amax > 0, np.frexp(amax)[1] - 1 + 127, 0) - down, 1)
    scale = np.exp2(byte - 127.0)
    codes = (blocks / scale).astype(np.float32).astype(dtype).astype(np.float64)
    return np.moveaxis((codes * scale).reshape(v.shape), -1, axis)


WIDE = False


def mx_kscale(k):
    if not WIDE:
        return np.ones(k)
    levels = np.array([10, -10, 5, -5, 0])
    a = np.random.permutation(np.resize(levels, k // 512 * 4)).reshape(k // 512, 4)
    idx = np.arange(k)
    return np.exp2(a[idx // 512, idx % 128 // 32])


BF16 = ml_dtypes.bfloat16


def bf(x):
    return np.asarray(x, np.float32).astype(BF16)


def f64(x):
    return np.asarray(x).astype(np.float64)


E2M1 = np.array([0.0, 0.5, 1.0, 1.5, 2.0, 3.0, 4.0, 6.0, -0.0, -0.5, -1.0, -1.5, -2.0, -3.0, -4.0, -6.0])


def pack_weight(w, fmt):
    k, n = w.shape
    w = f64(bf(w)).reshape(k // 32, 32, n)
    amax = np.abs(w).max(1)
    if fmt == "e4m3":
        byte = np.frexp(amax)[1] - 1 + 127 - 7
    else:
        mant, ex = np.frexp(amax / 6.0)
        byte = np.where(mant > 0.5, ex, ex - 1) + 127
    byte = np.clip(np.where(amax > 0, byte, 1), 1, 254)
    scaled = (w * np.exp2(127.0 - byte)[:, None, :]).reshape(k, n).astype(np.float32)
    by_word = np.ascontiguousarray(scaled.reshape(k // 512, 128, 4, n).transpose(0, 1, 3, 2))
    if fmt == "e4m3":
        words = by_word.astype(ml_dtypes.float8_e4m3fn).view(np.uint8)
    else:
        c = by_word.astype(ml_dtypes.float4_e2m1fn).view(np.uint8) & 0xF
        words = c[..., 0::2] | (c[..., 1::2] << 4)
    return np.ascontiguousarray(words), np.ascontiguousarray(byte.astype(np.uint8).reshape(k // 512, 16, n))


def unpack_weight(words, scales, fmt):
    g, p, n, _ = words.shape
    if fmt == "e4m3":
        vals = np.ascontiguousarray(words).view(ml_dtypes.float8_e4m3fn).astype(np.float64)
    else:
        nib = np.empty((g, p, n, 4), np.uint8)
        nib[..., 0::2] = words & 0xF
        nib[..., 1::2] = words >> 4
        vals = E2M1[nib]
    vals = vals * np.repeat(np.exp2(scales.astype(np.float64) - 127.0), 8, axis=1)[..., None]
    return vals.transpose(0, 1, 3, 2).reshape(g * 512, n)

def pack4(w):
    words, scales = pack_weight(w, "e2m1")
    return words.reshape(words.shape[0], 128, -1), scales


def unpack4(words, scales):
    return unpack_weight(words.reshape(words.shape[0], 128, -1, 2), scales, "e2m1")


B, DS, HH, WW, HID, HL, REP, GRP = 2, 32, 16, 16, 1024, 1024, 8, 4
C = 2 * DS
CN = REP * C


def elu(v):
    return np.where(v > 0.0, v, np.exp(np.minimum(v, 0.0)) - 1.0)


def neighbor_sum(x):
    xp = np.pad(x, ((0, 0), (0, 0), (1, 1), (1, 1)))
    full = sum(xp[:, :, di:di + HH, dj:dj + WW] for di in range(3) for dj in range(3))
    return full - x


def to_rows(t):
    return t.transpose(0, 2, 3, 1).reshape(B * HH * WW, t.shape[1])


def to_maps(r):
    return r.reshape(B, HH, WW, r.shape[1]).transpose(0, 3, 1, 2)


def setup_inputs():
    sc = mx_kscale(CN)[::REP]
    x_cat = bf(np.random.standard_normal((B, C, HH, WW)) * 0.4 * sc[None, :, None, None])
    w1 = np.random.standard_normal((HID, CN)) / np.sqrt(CN) / np.repeat(sc, REP)[None, :]
    words, scales = pack4(np.ascontiguousarray(w1.T))
    return {"x_cat": x_cat, "w1_words": words, "w1_scales": scales}


def reference(x_cat, w1_words, w1_scales):
    nbr = neighbor_sum(f64(x_cat))
    xn = np.repeat(nbr, REP, axis=1)
    z = mxq(to_rows(xn), 1, "e4m3") @ unpack4(w1_words, w1_scales)
    return to_maps(elu(z))

@@ -1,0 +1,114 @@
+from contextlib import ExitStack
+
+import concourse.mybir as mybir
+
+F32 = mybir.dt.float32
+BF16 = mybir.dt.bfloat16
+I32 = mybir.dt.int32
+U32 = mybir.dt.uint32
+U8 = mybir.dt.uint8
+FP8X4 = mybir.dt.float8_e4m3fn_x4
+FP4X4 = mybir.dt.float4_e2m1fn_x4
+ALU = mybir.AluOpType
+ACT = mybir.ActivationFunctionType
+
+P = 128
+PACK = 4
+B, C, H, W = 2, 64, 16, 16
+REP = 8
+HID = 1024
+NPIX = B * H * W
+COPIES = P // C
+M_TILES = HID // P
+FP4_WORD_BYTES = 2
+
+VECTOR_PIX = 3 * NPIX // 4
+
+FLOPS = 2 * NPIX * C * REP * HID
+
+
+def tile_qca_operator_deep_pa_s_kernel(tc, x_cat, w1_words, w1_scales, out):
+    nc = tc.nc
+    with ExitStack() as ctx:
+        keep = ctx.enter_context(tc.tile_pool(name="keep", bufs=1))
+        work = ctx.enter_context(tc.tile_pool(name="work", bufs=M_TILES))
+        psum = ctx.enter_context(tc.psum_pool(name="psum", bufs=M_TILES))
+
+        x_rows = keep.tile([P, B, H + 2, W], BF16)
+        x_by_channel = x_cat.rearrange("b c h w -> c b h w")
+        nc.sync.dma_start(out=x_rows[0:P:COPIES, :, 1 : H + 1, :], in_=x_by_channel)
+        nc.scalar.dma_start(out=x_rows[1:P:COPIES, :, 1 : H + 1, :], in_=x_by_channel)
+        nc.vector.memset(x_rows[:, :, 0 : H + 2 : H + 1, :], 0.0)
+
+        w_words = keep.tile([P, HID * FP4_WORD_BYTES], U8, align_bytes=64)
+        nc.sync.dma_start(out=w_words[:].bitcast(I32), in_=w1_words[0].bitcast(I32))
+
+        w_scales = keep.tile([P, HID], U8, align_bytes=64)
+        nc.vector.memset(w_scales[:].bitcast(I32), 0)
+        for quadrant in range(4):
+            nc.sync.dma_start(
+                out=w_scales[32 * quadrant : 32 * quadrant + 4, :].bitcast(I32),
+                in_=w1_scales[0, 4 * quadrant : 4 * quadrant + 4, :].bitcast(I32),
+            )
+
+        warm = keep.tile([P, 1], F32)
+        nc.vector.memset(warm[:], 0.0)
+        nc.scalar.activation(out=warm[:], in_=warm[:], func=ACT.Exp)
+
+        above_below = keep.tile([P, B, H, W], F32)
+        nc.vector.tensor_tensor(
+            out=above_below[:], in0=x_rows[:, :, 0:H, :], in1=x_rows[:, :, 2 : H + 2, :], op=ALU.add
+        )
+        column3 = keep.tile([P, B, H, W + 2], F32)
+        nc.vector.memset(column3[:, :, :, 0 : W + 2 : W + 1], 0.0)
+        nc.vector.tensor_tensor(
+            out=column3[:, :, :, 1 : W + 1], in0=above_below[:], in1=x_rows[:, :, 1 : H + 1, :], op=ALU.add
+        )
+        left_right = keep.tile([P, B, H, W], F32)
+        nc.vector.tensor_tensor(
+            out=left_right[:], in0=column3[:, :, :, 0:W], in1=column3[:, :, :, 2 : W + 2], op=ALU.add
+        )
+        nbr = keep.tile([P, B, H, W], BF16)
+        nc.vector.tensor_tensor(out=nbr[:], in0=left_right[:], in1=above_below[:], op=ALU.add)
+
+        nbr_pix = nbr[:].rearrange("p b h w -> p (b h w)")
+        xn4 = keep.tile([P, NPIX, PACK], BF16, align_bytes=64)
+        nc.vector.tensor_copy(
+            out=xn4[:, 0:VECTOR_PIX, :],
+            in_=nbr_pix[:, 0:VECTOR_PIX].unsqueeze(2).to_broadcast([P, VECTOR_PIX, PACK]),
+        )
+        nc.scalar.copy(
+            out=xn4[:, VECTOR_PIX:NPIX, :],
+            in_=nbr_pix[:, VECTOR_PIX:NPIX].unsqueeze(2).to_broadcast([P, NPIX - VECTOR_PIX, PACK]),
+        )
+        x_words = keep.tile([P, NPIX], U32, align_bytes=64)
+        x_scales = keep.tile([P, NPIX], U8, align_bytes=64)
+        nc.vector.quantize_mx(
+            out=x_words[:].bitcast(FP8X4),
+            scales=x_scales[:],
+            in_=xn4[:].rearrange("p w t -> p (w t)"),
+        )
+
+        out_tiles = out.rearrange("b (m p) h w -> m p b (h w)", p=P)
+        for m in range(M_TILES):
+            z = psum.tile([P, NPIX], F32)
+            nc.tensor.matmul_mx(
+                out=z[:],
+                lhsT=w_words[:, m * P * FP4_WORD_BYTES : (m + 1) * P * FP4_WORD_BYTES].bitcast(FP4X4),
+                lhsT_scale=w_scales[:, m * P : (m + 1) * P],
+                rhs=x_words[:].bitcast(FP8X4),
+                rhs_scale=x_scales[:],
+                start=True,
+                stop=True,
+            )
+            exp_z = work.tile([P, NPIX], F32)
+            nc.scalar.activation(out=exp_z[:], in_=z[:], func=ACT.Exp)
+            negative_part = work.tile([P, NPIX], F32)
+            nc.vector.tensor_scalar(
+                out=negative_part[:], in0=exp_z[:], scalar1=1.0, scalar2=1.0, op0=ALU.min, op1=ALU.subtract
+            )
+            elu = work.tile([P, NPIX], F32)
+            nc.vector.scalar_tensor_tensor(
+                out=elu[:], in0=z[:], scalar=0.0, in1=negative_part[:], op0=ALU.max, op1=ALU.add
+            )
+            nc.sync.dma_start(out=out_tiles[m], in_=elu[:].rearrange("p (b x) -> p b x", b=B))

@@ -24,6 +24,8 @@ FP4_WORD_BYTES = 2
 
 VECTOR_PIX = 3 * NPIX // 4
 
+CLAMP_ROUND = 4
+
 FLOPS = 2 * NPIX * C * REP * HID
 
 
@@ -104,7 +106,8 @@ def tile_qca_operator_deep_pa_s_kernel(tc, x_cat, w1_words, w1_scales, out):
             exp_z = work.tile([P, NPIX], F32)
             nc.scalar.activation(out=exp_z[:], in_=z[:], func=ACT.Exp)
             negative_part = work.tile([P, NPIX], F32)
-            nc.vector.tensor_scalar(
+            clamp_engine = nc.vector if m % CLAMP_ROUND == 0 else nc.gpsimd
+            clamp_engine.tensor_scalar(
                 out=negative_part[:], in0=exp_z[:], scalar1=1.0, scalar2=1.0, op0=ALU.min, op1=ALU.subtract
             )
             elu = work.tile([P, NPIX], F32)

@@ -22,9 +22,9 @@ COPIES = P // C
 M_TILES = HID // P
 FP4_WORD_BYTES = 2
 
-VECTOR_PIX = 3 * NPIX // 4
+SCALAR_PIX = 3 * H * W // 4
 
-CLAMP_ROUND = 4
+MINUS_ONE_ROUND = 4
 
 FLOPS = 2 * NPIX * C * REP * HID
 
@@ -39,7 +39,7 @@ def tile_qca_operator_deep_pa_s_kernel(tc, x_cat, w1_words, w1_scales, out):
         x_rows = keep.tile([P, B, H + 2, W], BF16)
         x_by_channel = x_cat.rearrange("b c h w -> c b h w")
         nc.sync.dma_start(out=x_rows[0:P:COPIES, :, 1 : H + 1, :], in_=x_by_channel)
-        nc.scalar.dma_start(out=x_rows[1:P:COPIES, :, 1 : H + 1, :], in_=x_by_channel)
+        nc.sync.dma_start(out=x_rows[1:P:COPIES, :, 1 : H + 1, :], in_=x_by_channel)
         nc.vector.memset(x_rows[:, :, 0 : H + 2 : H + 1, :], 0.0)
 
         w_words = keep.tile([P, HID * FP4_WORD_BYTES], U8, align_bytes=64)
@@ -58,30 +58,34 @@ def tile_qca_operator_deep_pa_s_kernel(tc, x_cat, w1_words, w1_scales, out):
         nc.scalar.activation(out=warm[:], in_=warm[:], func=ACT.Exp)
 
         above_below = keep.tile([P, B, H, W], F32)
-        nc.vector.tensor_tensor(
-            out=above_below[:], in0=x_rows[:, :, 0:H, :], in1=x_rows[:, :, 2 : H + 2, :], op=ALU.add
-        )
         column3 = keep.tile([P, B, H, W + 2], F32)
-        nc.vector.memset(column3[:, :, :, 0 : W + 2 : W + 1], 0.0)
-        nc.vector.tensor_tensor(
-            out=column3[:, :, :, 1 : W + 1], in0=above_below[:], in1=x_rows[:, :, 1 : H + 1, :], op=ALU.add
-        )
         left_right = keep.tile([P, B, H, W], F32)
-        nc.vector.tensor_tensor(
-            out=left_right[:], in0=column3[:, :, :, 0:W], in1=column3[:, :, :, 2 : W + 2], op=ALU.add
-        )
         nbr = keep.tile([P, B, H, W], BF16)
-        nc.vector.tensor_tensor(out=nbr[:], in0=left_right[:], in1=above_below[:], op=ALU.add)
+        nc.vector.memset(column3[:, :, :, 0 : W + 2 : W + 1], 0.0)
+        for b in range(B):
+            nc.vector.tensor_tensor(
+                out=above_below[:, b], in0=x_rows[:, b, 0:H, :], in1=x_rows[:, b, 2 : H + 2, :], op=ALU.add
+            )
+        for b in range(B):
+            nc.vector.tensor_tensor(
+                out=column3[:, b, :, 1 : W + 1], in0=above_below[:, b], in1=x_rows[:, b, 1 : H + 1, :], op=ALU.add
+            )
+        for b in range(B):
+            nc.vector.tensor_tensor(
+                out=left_right[:, b], in0=column3[:, b, :, 0:W], in1=column3[:, b, :, 2 : W + 2], op=ALU.add
+            )
+        for b in range(B):
+            nc.vector.tensor_tensor(out=nbr[:, b], in0=left_right[:, b], in1=above_below[:, b], op=ALU.add)
 
         nbr_pix = nbr[:].rearrange("p b h w -> p (b h w)")
         xn4 = keep.tile([P, NPIX, PACK], BF16, align_bytes=64)
-        nc.vector.tensor_copy(
-            out=xn4[:, 0:VECTOR_PIX, :],
-            in_=nbr_pix[:, 0:VECTOR_PIX].unsqueeze(2).to_broadcast([P, VECTOR_PIX, PACK]),
-        )
         nc.scalar.copy(
-            out=xn4[:, VECTOR_PIX:NPIX, :],
-            in_=nbr_pix[:, VECTOR_PIX:NPIX].unsqueeze(2).to_broadcast([P, NPIX - VECTOR_PIX, PACK]),
+            out=xn4[:, 0:SCALAR_PIX, :],
+            in_=nbr_pix[:, 0:SCALAR_PIX].unsqueeze(2).to_broadcast([P, SCALAR_PIX, PACK]),
+        )
+        nc.vector.tensor_copy(
+            out=xn4[:, SCALAR_PIX:NPIX, :],
+            in_=nbr_pix[:, SCALAR_PIX:NPIX].unsqueeze(2).to_broadcast([P, NPIX - SCALAR_PIX, PACK]),
         )
         x_words = keep.tile([P, NPIX], U32, align_bytes=64)
         x_scales = keep.tile([P, NPIX], U8, align_bytes=64)
@@ -105,13 +109,13 @@ def tile_qca_operator_deep_pa_s_kernel(tc, x_cat, w1_words, w1_scales, out):
             )
             exp_z = work.tile([P, NPIX], F32)
             nc.scalar.activation(out=exp_z[:], in_=z[:], func=ACT.Exp)
-            negative_part = work.tile([P, NPIX], F32)
-            clamp_engine = nc.vector if m % CLAMP_ROUND == 0 else nc.gpsimd
-            clamp_engine.tensor_scalar(
-                out=negative_part[:], in0=exp_z[:], scalar1=1.0, scalar2=1.0, op0=ALU.min, op1=ALU.subtract
+            exp_m1 = work.tile([P, NPIX], F32)
+            minus_one_engine = nc.vector if m % MINUS_ONE_ROUND == 0 else nc.gpsimd
+            minus_one_engine.tensor_scalar(
+                out=exp_m1[:], in0=exp_z[:], scalar1=1.0, scalar2=-1.0, op0=ALU.mult, op1=ALU.add
             )
             elu = work.tile([P, NPIX], F32)
             nc.vector.scalar_tensor_tensor(
-                out=elu[:], in0=z[:], scalar=0.0, in1=negative_part[:], op0=ALU.max, op1=ALU.add
+                out=elu[:], in0=exp_m1[:], scalar=0.0, in1=z[:], op0=ALU.min, op1=ALU.max
             )
             nc.sync.dma_start(out=out_tiles[m], in_=elu[:].rearrange("p (b x) -> p b x", b=B))

@@ -17,29 +17,31 @@ PACK = 4
 B, C, H, W = 2, 64, 16, 16
 REP = 8
 HID = 1024
-NPIX = B * H * W
+PIX = H * W
 COPIES = P // C
-M_TILES = HID // P
 FP4_WORD_BYTES = 2
+BANK_F32 = 512
+PAIR = BANK_F32 // PIX
+PAIRS = HID // (P * PAIR)
 
-SCALAR_PIX = 3 * H * W // 4
+SCALAR_PIX = PIX // 2
 
 MINUS_ONE_ROUND = 4
 
-FLOPS = 2 * NPIX * C * REP * HID
+FLOPS = 2 * B * PIX * C * REP * HID
 
 
 def tile_qca_operator_deep_pa_s_kernel(tc, x_cat, w1_words, w1_scales, out):
     nc = tc.nc
     with ExitStack() as ctx:
         keep = ctx.enter_context(tc.tile_pool(name="keep", bufs=1))
-        work = ctx.enter_context(tc.tile_pool(name="work", bufs=M_TILES))
-        psum = ctx.enter_context(tc.psum_pool(name="psum", bufs=M_TILES))
+        work = ctx.enter_context(tc.tile_pool(name="work", bufs=B * PAIRS))
+        psum = ctx.enter_context(tc.psum_pool(name="psum", bufs=B * PAIRS))
 
         x_rows = keep.tile([P, B, H + 2, W], BF16)
         x_by_channel = x_cat.rearrange("b c h w -> c b h w")
-        nc.sync.dma_start(out=x_rows[0:P:COPIES, :, 1 : H + 1, :], in_=x_by_channel)
-        nc.sync.dma_start(out=x_rows[1:P:COPIES, :, 1 : H + 1, :], in_=x_by_channel)
+        for copy in range(COPIES):
+            nc.sync.dma_start(out=x_rows[copy:P:COPIES, :, 1 : H + 1, :], in_=x_by_channel)
         nc.vector.memset(x_rows[:, :, 0 : H + 2 : H + 1, :], 0.0)
 
         w_words = keep.tile([P, HID * FP4_WORD_BYTES], U8, align_bytes=64)
@@ -77,45 +79,49 @@ def tile_qca_operator_deep_pa_s_kernel(tc, x_cat, w1_words, w1_scales, out):
         for b in range(B):
             nc.vector.tensor_tensor(out=nbr[:, b], in0=left_right[:, b], in1=above_below[:, b], op=ALU.add)
 
-        nbr_pix = nbr[:].rearrange("p b h w -> p (b h w)")
-        xn4 = keep.tile([P, NPIX, PACK], BF16, align_bytes=64)
-        nc.scalar.copy(
-            out=xn4[:, 0:SCALAR_PIX, :],
-            in_=nbr_pix[:, 0:SCALAR_PIX].unsqueeze(2).to_broadcast([P, SCALAR_PIX, PACK]),
-        )
-        nc.vector.tensor_copy(
-            out=xn4[:, SCALAR_PIX:NPIX, :],
-            in_=nbr_pix[:, SCALAR_PIX:NPIX].unsqueeze(2).to_broadcast([P, NPIX - SCALAR_PIX, PACK]),
-        )
-        x_words = keep.tile([P, NPIX], U32, align_bytes=64)
-        x_scales = keep.tile([P, NPIX], U8, align_bytes=64)
-        nc.vector.quantize_mx(
-            out=x_words[:].bitcast(FP8X4),
-            scales=x_scales[:],
-            in_=xn4[:].rearrange("p w t -> p (w t)"),
-        )
+        nbr_pix = nbr[:].rearrange("p b h w -> p b (h w)")
+        xn4 = keep.tile([P, B, PIX, PACK], BF16, align_bytes=64)
+        x_words = keep.tile([P, B, PIX], U32, align_bytes=64)
+        x_scales = keep.tile([P, B, PIX], U8, align_bytes=64)
+        for b in range(B):
+            nc.scalar.copy(
+                out=xn4[:, b, 0:SCALAR_PIX, :],
+                in_=nbr_pix[:, b, 0:SCALAR_PIX].unsqueeze(2).to_broadcast([P, SCALAR_PIX, PACK]),
+            )
+            nc.vector.tensor_copy(
+                out=xn4[:, b, SCALAR_PIX:PIX, :],
+                in_=nbr_pix[:, b, SCALAR_PIX:PIX].unsqueeze(2).to_broadcast([P, PIX - SCALAR_PIX, PACK]),
+            )
+            nc.vector.quantize_mx(
+                out=x_words[:, b, :].bitcast(FP8X4),
+                scales=x_scales[:, b, :],
+                in_=xn4[:, b].rearrange("p w t -> p (w t)"),
+            )
 
-        out_tiles = out.rearrange("b (m p) h w -> m p b (h w)", p=P)
-        for m in range(M_TILES):
-            z = psum.tile([P, NPIX], F32)
-            nc.tensor.matmul_mx(
-                out=z[:],
-                lhsT=w_words[:, m * P * FP4_WORD_BYTES : (m + 1) * P * FP4_WORD_BYTES].bitcast(FP4X4),
-                lhsT_scale=w_scales[:, m * P : (m + 1) * P],
-                rhs=x_words[:].bitcast(FP8X4),
-                rhs_scale=x_scales[:],
-                start=True,
-                stop=True,
-            )
-            exp_z = work.tile([P, NPIX], F32)
-            nc.scalar.activation(out=exp_z[:], in_=z[:], func=ACT.Exp)
-            exp_m1 = work.tile([P, NPIX], F32)
-            minus_one_engine = nc.vector if m % MINUS_ONE_ROUND == 0 else nc.gpsimd
-            minus_one_engine.tensor_scalar(
-                out=exp_m1[:], in0=exp_z[:], scalar1=1.0, scalar2=-1.0, op0=ALU.mult, op1=ALU.add
-            )
-            elu = work.tile([P, NPIX], F32)
-            nc.vector.scalar_tensor_tensor(
-                out=elu[:], in0=exp_m1[:], scalar=0.0, in1=z[:], op0=ALU.min, op1=ALU.max
-            )
-            nc.sync.dma_start(out=out_tiles[m], in_=elu[:].rearrange("p (b x) -> p b x", b=B))
+        out_banks = out.rearrange("b (j i p) h w -> b j p i (h w)", i=PAIR, p=P)
+        for b in range(B):
+            for j in range(PAIRS):
+                z = psum.tile([P, PAIR, PIX], F32)
+                for i in range(PAIR):
+                    m = j * PAIR + i
+                    nc.tensor.matmul_mx(
+                        out=z[:, i, :],
+                        lhsT=w_words[:, m * P * FP4_WORD_BYTES : (m + 1) * P * FP4_WORD_BYTES].bitcast(FP4X4),
+                        lhsT_scale=w_scales[:, m * P : (m + 1) * P],
+                        rhs=x_words[:, b, :].bitcast(FP8X4),
+                        rhs_scale=x_scales[:, b, :],
+                        start=True,
+                        stop=True,
+                    )
+                exp_z = work.tile([P, PAIR, PIX], F32)
+                nc.scalar.activation(out=exp_z[:], in_=z[:], func=ACT.Exp)
+                exp_m1 = work.tile([P, PAIR, PIX], F32)
+                minus_one_engine = nc.vector if (b * PAIRS + j) % MINUS_ONE_ROUND == 0 else nc.gpsimd
+                minus_one_engine.tensor_scalar(
+                    out=exp_m1[:], in0=exp_z[:], scalar1=1.0, scalar2=-1.0, op0=ALU.mult, op1=ALU.add
+                )
+                elu = work.tile([P, PAIR, PIX], F32)
+                nc.vector.scalar_tensor_tensor(
+                    out=elu[:], in0=exp_m1[:], scalar=0.0, in1=z[:], op0=ALU.min, op1=ALU.max
+                )
+                nc.sync.dma_start(out=out_banks[b, j], in_=elu[:])

@@ -23,10 +23,11 @@ FP4_WORD_BYTES = 2
 BANK_F32 = 512
 PAIR = BANK_F32 // PIX
 PAIRS = HID // (P * PAIR)
+BANKS = 8
 
-SCALAR_PIX = PIX // 2
+SCALAR_PIX = 96
 
-MINUS_ONE_ROUND = 4
+VECTOR_MINUS_ONE = (0, 4)
 
 FLOPS = 2 * B * PIX * C * REP * HID
 
@@ -36,13 +37,19 @@ def tile_qca_operator_deep_pa_s_kernel(tc, x_cat, w1_words, w1_scales, out):
     with ExitStack() as ctx:
         keep = ctx.enter_context(tc.tile_pool(name="keep", bufs=1))
         work = ctx.enter_context(tc.tile_pool(name="work", bufs=B * PAIRS))
-        psum = ctx.enter_context(tc.psum_pool(name="psum", bufs=B * PAIRS))
+        psum = ctx.enter_context(tc.psum_pool(name="psum", bufs=BANKS))
 
-        x_rows = keep.tile([P, B, H + 2, W], BF16)
         x_by_channel = x_cat.rearrange("b c h w -> c b h w")
+
+        x_updown = keep.tile([P, B, H, W], BF16)
+        nc.sync.dma_start(out=x_updown[0:C, :, 1:H, :], in_=x_by_channel[:, :, 0 : H - 1, :])
+        nc.sync.dma_start(out=x_updown[C:P, :, 0 : H - 1, :], in_=x_by_channel[:, :, 1:H, :])
+        nc.vector.memset(x_updown[0:C, :, 0:1, :], 0.0)
+        nc.vector.memset(x_updown[C:P, :, H - 1 : H, :], 0.0)
+
+        x_twice = keep.tile([P, B, H, W], BF16)
         for copy in range(COPIES):
-            nc.sync.dma_start(out=x_rows[copy:P:COPIES, :, 1 : H + 1, :], in_=x_by_channel)
-        nc.vector.memset(x_rows[:, :, 0 : H + 2 : H + 1, :], 0.0)
+            nc.sync.dma_start(out=x_twice[copy:P:COPIES], in_=x_by_channel)
 
         w_words = keep.tile([P, HID * FP4_WORD_BYTES], U8, align_bytes=64)
         nc.sync.dma_start(out=w_words[:].bitcast(I32), in_=w1_words[0].bitcast(I32))
@@ -59,31 +66,45 @@ def tile_qca_operator_deep_pa_s_kernel(tc, x_cat, w1_words, w1_scales, out):
         nc.vector.memset(warm[:], 0.0)
         nc.scalar.activation(out=warm[:], in_=warm[:], func=ACT.Exp)
 
-        above_below = keep.tile([P, B, H, W], F32)
-        column3 = keep.tile([P, B, H, W + 2], F32)
-        left_right = keep.tile([P, B, H, W], F32)
-        nbr = keep.tile([P, B, H, W], BF16)
-        nc.vector.memset(column3[:, :, :, 0 : W + 2 : W + 1], 0.0)
-        for b in range(B):
-            nc.vector.tensor_tensor(
-                out=above_below[:, b], in0=x_rows[:, b, 0:H, :], in1=x_rows[:, b, 2 : H + 2, :], op=ALU.add
+        pick = keep.tile([P, P], BF16)
+        nc.gpsimd.memset(pick[:], 0.0)
+        for half in range(2):
+            nc.gpsimd.affine_select(
+                out=pick[:],
+                in_=pick[:],
+                compare_op=ALU.not_equal,
+                fill=1.0,
+                base=-C * half,
+                pattern=[[-1, C], [0, COPIES]],
+                channel_multiplier=1,
             )
-        for b in range(B):
-            nc.vector.tensor_tensor(
-                out=column3[:, b, :, 1 : W + 1], in0=above_below[:, b], in1=x_rows[:, b, 1 : H + 1, :], op=ALU.add
-            )
-        for b in range(B):
-            nc.vector.tensor_tensor(
-                out=left_right[:, b], in0=column3[:, b, :, 0:W], in1=column3[:, b, :, 2 : W + 2], op=ALU.add
-            )
-        for b in range(B):
-            nc.vector.tensor_tensor(out=nbr[:, b], in0=left_right[:, b], in1=above_below[:, b], op=ALU.add)
+        pick_cols = pick[:]
 
+        sides = keep.tile([P, B, H, W], F32)
+        for b in range(B):
+            nc.vector.tensor_tensor(
+                out=sides[:, b, :, 1 : W - 1], in0=x_twice[:, b, :, 0 : W - 2], in1=x_twice[:, b, :, 2:W], op=ALU.add
+            )
+        nc.scalar.copy(out=sides[:, :, :, 0 : W : W - 1], in_=x_twice[:, :, :, 1 : W - 1 : W - 3])
+
+        nbr = keep.tile([P, B, H, W], BF16)
         nbr_pix = nbr[:].rearrange("p b h w -> p b (h w)")
         xn4 = keep.tile([P, B, PIX, PACK], BF16, align_bytes=64)
         x_words = keep.tile([P, B, PIX], U32, align_bytes=64)
         x_scales = keep.tile([P, B, PIX], U8, align_bytes=64)
-        for b in range(B):
+
+        def neighbour_sum(b):
+            six = psum.tile([P, H, W], F32, name="six", tag="bank")
+            nc.tensor.matmul(out=six[:], lhsT=pick_cols, rhs=x_updown[:, b], start=True, stop=False)
+            nc.tensor.matmul(
+                out=six[:, :, 1:W], lhsT=pick_cols, rhs=x_updown[:, b, :, 0 : W - 1], start=False, stop=False
+            )
+            nc.tensor.matmul(
+                out=six[:, :, 0 : W - 1], lhsT=pick_cols, rhs=x_updown[:, b, :, 1:W], start=False, stop=True
+            )
+            nc.vector.tensor_tensor(out=nbr[:, b], in0=six[:], in1=sides[:, b], op=ALU.add)
+
+        def repeat(b):
             nc.scalar.copy(
                 out=xn4[:, b, 0:SCALAR_PIX, :],
                 in_=nbr_pix[:, b, 0:SCALAR_PIX].unsqueeze(2).to_broadcast([P, SCALAR_PIX, PACK]),
@@ -92,36 +113,60 @@ def tile_qca_operator_deep_pa_s_kernel(tc, x_cat, w1_words, w1_scales, out):
                 out=xn4[:, b, SCALAR_PIX:PIX, :],
                 in_=nbr_pix[:, b, SCALAR_PIX:PIX].unsqueeze(2).to_broadcast([P, PIX - SCALAR_PIX, PACK]),
             )
+
+        def quantise(b):
             nc.vector.quantize_mx(
                 out=x_words[:, b, :].bitcast(FP8X4),
                 scales=x_scales[:, b, :],
                 in_=xn4[:, b].rearrange("p w t -> p (w t)"),
             )
 
+        with tc.manual_schedule(engines={mybir.EngineType.DVE}):
+            neighbour_sum(0)
+            repeat(0)
+            neighbour_sum(1)
+            quantise(0)
+            repeat(1)
+            quantise(1)
+
         out_banks = out.rearrange("b (j i p) h w -> b j p i (h w)", i=PAIR, p=P)
-        for b in range(B):
-            for j in range(PAIRS):
-                z = psum.tile([P, PAIR, PIX], F32)
-                for i in range(PAIR):
-                    m = j * PAIR + i
-                    nc.tensor.matmul_mx(
-                        out=z[:, i, :],
-                        lhsT=w_words[:, m * P * FP4_WORD_BYTES : (m + 1) * P * FP4_WORD_BYTES].bitcast(FP4X4),
-                        lhsT_scale=w_scales[:, m * P : (m + 1) * P],
-                        rhs=x_words[:, b, :].bitcast(FP8X4),
-                        rhs_scale=x_scales[:, b, :],
-                        start=True,
-                        stop=True,
-                    )
-                exp_z = work.tile([P, PAIR, PIX], F32)
-                nc.scalar.activation(out=exp_z[:], in_=z[:], func=ACT.Exp)
-                exp_m1 = work.tile([P, PAIR, PIX], F32)
-                minus_one_engine = nc.vector if (b * PAIRS + j) % MINUS_ONE_ROUND == 0 else nc.gpsimd
-                minus_one_engine.tensor_scalar(
-                    out=exp_m1[:], in0=exp_z[:], scalar1=1.0, scalar2=-1.0, op0=ALU.mult, op1=ALU.add
+        z_of = {}
+        exp_m1_of = {}
+
+        def passes_and_exp(n):
+            b, j = divmod(n, PAIRS)
+            z = psum.tile([P, PAIR, PIX], F32, name="z", tag="bank")
+            for i in range(PAIR):
+                m = j * PAIR + i
+                nc.tensor.matmul_mx(
+                    out=z[:, i, :],
+                    lhsT=w_words[:, m * P * FP4_WORD_BYTES : (m + 1) * P * FP4_WORD_BYTES].bitcast(FP4X4),
+                    lhsT_scale=w_scales[:, m * P : (m + 1) * P],
+                    rhs=x_words[:, b, :].bitcast(FP8X4),
+                    rhs_scale=x_scales[:, b, :],
+                    start=True,
+                    stop=True,
                 )
-                elu = work.tile([P, PAIR, PIX], F32)
-                nc.vector.scalar_tensor_tensor(
-                    out=elu[:], in0=exp_m1[:], scalar=0.0, in1=z[:], op0=ALU.min, op1=ALU.max
-                )
-                nc.sync.dma_start(out=out_banks[b, j], in_=elu[:])
+            exp_z = work.tile([P, PAIR, PIX], F32, name="exp_z")
+            nc.scalar.activation(out=exp_z[:], in_=z[:], func=ACT.Exp)
+            exp_m1 = work.tile([P, PAIR, PIX], F32, name="exp_m1")
+            minus_one_engine = nc.vector if n in VECTOR_MINUS_ONE else nc.gpsimd
+            minus_one_engine.tensor_scalar(
+                out=exp_m1[:], in0=exp_z[:], scalar1=1.0, scalar2=-1.0, op0=ALU.mult, op1=ALU.add
+            )
+            z_of[n] = z
+            exp_m1_of[n] = exp_m1
+
+        def finish_and_store(n):
+            b, j = divmod(n, PAIRS)
+            elu = work.tile([P, PAIR, PIX], F32, name="elu")
+            nc.vector.scalar_tensor_tensor(
+                out=elu[:], in0=exp_m1_of[n][:], scalar=0.0, in1=z_of[n][:], op0=ALU.min, op1=ALU.max
+            )
+            nc.sync.dma_start(out=out_banks[b, j], in_=elu[:])
+
+        passes_and_exp(0)
+        for n in range(1, B * PAIRS):
+            passes_and_exp(n)
+            finish_and_store(n - 1)
+        finish_and_store(B * PAIRS - 1)

@@ -23,9 +23,12 @@ FP4_WORD_BYTES = 2
 BANK_F32 = 512
 PAIR = BANK_F32 // PIX
 PAIRS = HID // (P * PAIR)
+TILES = HID // P
+HALF_ROWS = H // 2
+HALF_PIX = PIX // 2
 BANKS = 8
 
-SCALAR_PIX = 96
+SCALAR_SHARE_OF_8 = 3
 
 VECTOR_MINUS_ONE = (0, 4)
 
@@ -93,80 +96,90 @@ def tile_qca_operator_deep_pa_s_kernel(tc, x_cat, w1_words, w1_scales, out):
         x_words = keep.tile([P, B, PIX], U32, align_bytes=64)
         x_scales = keep.tile([P, B, PIX], U8, align_bytes=64)
 
-        def neighbour_sum(b):
-            six = psum.tile([P, H, W], F32, name="six", tag="bank")
-            nc.tensor.matmul(out=six[:], lhsT=pick_cols, rhs=x_updown[:, b], start=True, stop=False)
-            nc.tensor.matmul(
-                out=six[:, :, 1:W], lhsT=pick_cols, rhs=x_updown[:, b, :, 0 : W - 1], start=False, stop=False
+        def neighbour_sum(b, row0, rows):
+            part = x_updown[:, b, row0 : row0 + rows, :]
+            six = psum.tile([P, rows, W], F32, name="six", tag="bank")
+            nc.tensor.matmul(out=six[:], lhsT=pick_cols, rhs=part, start=True, stop=False)
+            nc.tensor.matmul(out=six[:, :, 1:W], lhsT=pick_cols, rhs=part[:, :, 0 : W - 1], start=False, stop=False)
+            nc.tensor.matmul(out=six[:, :, 0 : W - 1], lhsT=pick_cols, rhs=part[:, :, 1:W], start=False, stop=True)
+            nc.vector.tensor_tensor(
+                out=nbr[:, b, row0 : row0 + rows, :], in0=six[:], in1=sides[:, b, row0 : row0 + rows, :], op=ALU.add
             )
-            nc.tensor.matmul(
-                out=six[:, :, 0 : W - 1], lhsT=pick_cols, rhs=x_updown[:, b, :, 1:W], start=False, stop=True
-            )
-            nc.vector.tensor_tensor(out=nbr[:, b], in0=six[:], in1=sides[:, b], op=ALU.add)
 
-        def repeat(b):
+        def repeat(b, pix0, pixels):
+            cut = pix0 + pixels * SCALAR_SHARE_OF_8 // 8
             nc.scalar.copy(
-                out=xn4[:, b, 0:SCALAR_PIX, :],
-                in_=nbr_pix[:, b, 0:SCALAR_PIX].unsqueeze(2).to_broadcast([P, SCALAR_PIX, PACK]),
+                out=xn4[:, b, pix0:cut, :], in_=nbr_pix[:, b, pix0:cut].unsqueeze(2).to_broadcast([P, cut - pix0, PACK])
             )
             nc.vector.tensor_copy(
-                out=xn4[:, b, SCALAR_PIX:PIX, :],
-                in_=nbr_pix[:, b, SCALAR_PIX:PIX].unsqueeze(2).to_broadcast([P, PIX - SCALAR_PIX, PACK]),
+                out=xn4[:, b, cut : pix0 + pixels, :],
+                in_=nbr_pix[:, b, cut : pix0 + pixels].unsqueeze(2).to_broadcast([P, pix0 + pixels - cut, PACK]),
             )
 
-        def quantise(b):
+        def quantise(b, pix0, pixels):
             nc.vector.quantize_mx(
-                out=x_words[:, b, :].bitcast(FP8X4),
-                scales=x_scales[:, b, :],
-                in_=xn4[:, b].rearrange("p w t -> p (w t)"),
+                out=x_words[:, b, pix0 : pix0 + pixels].bitcast(FP8X4),
+                scales=x_scales[:, b, pix0 : pix0 + pixels],
+                in_=xn4[:, b, pix0 : pix0 + pixels, :].rearrange("p w t -> p (w t)"),
             )
 
         with tc.manual_schedule(engines={mybir.EngineType.DVE}):
-            neighbour_sum(0)
-            repeat(0)
-            neighbour_sum(1)
-            quantise(0)
-            repeat(1)
-            quantise(1)
+            neighbour_sum(0, 0, HALF_ROWS)
+            repeat(0, 0, HALF_PIX)
+            neighbour_sum(0, HALF_ROWS, HALF_ROWS)
+            quantise(0, 0, HALF_PIX)
+            repeat(0, HALF_PIX, HALF_PIX)
+            neighbour_sum(1, 0, H)
+            quantise(0, HALF_PIX, HALF_PIX)
+            repeat(1, 0, PIX)
+            quantise(1, 0, PIX)
 
-        out_banks = out.rearrange("b (j i p) h w -> b j p i (h w)", i=PAIR, p=P)
+        banks = [(b, m) for b in range(B) for m in range(0, TILES, PAIR)]
+        out_tiles = out.rearrange("b (m p) h w -> b p m (h w)", p=P)
         z_of = {}
         exp_m1_of = {}
 
-        def passes_and_exp(n):
-            b, j = divmod(n, PAIRS)
-            z = psum.tile([P, PAIR, PIX], F32, name="z", tag="bank")
+        def passes(n, pix0, pixels):
+            b, first = banks[n]
+            if n not in z_of:
+                z_of[n] = psum.tile([P, PAIR, PIX], F32, name="z", tag="bank")
             for i in range(PAIR):
-                m = j * PAIR + i
+                m = first + i
                 nc.tensor.matmul_mx(
-                    out=z[:, i, :],
+                    out=z_of[n][:, i, pix0 : pix0 + pixels],
                     lhsT=w_words[:, m * P * FP4_WORD_BYTES : (m + 1) * P * FP4_WORD_BYTES].bitcast(FP4X4),
                     lhsT_scale=w_scales[:, m * P : (m + 1) * P],
-                    rhs=x_words[:, b, :].bitcast(FP8X4),
-                    rhs_scale=x_scales[:, b, :],
+                    rhs=x_words[:, b, pix0 : pix0 + pixels].bitcast(FP8X4),
+                    rhs_scale=x_scales[:, b, pix0 : pix0 + pixels],
                     start=True,
                     stop=True,
                 )
+
+        def exp_minus_one(n):
             exp_z = work.tile([P, PAIR, PIX], F32, name="exp_z")
-            nc.scalar.activation(out=exp_z[:], in_=z[:], func=ACT.Exp)
+            nc.scalar.activation(out=exp_z[:], in_=z_of[n][:], func=ACT.Exp)
             exp_m1 = work.tile([P, PAIR, PIX], F32, name="exp_m1")
             minus_one_engine = nc.vector if n in VECTOR_MINUS_ONE else nc.gpsimd
             minus_one_engine.tensor_scalar(
                 out=exp_m1[:], in0=exp_z[:], scalar1=1.0, scalar2=-1.0, op0=ALU.mult, op1=ALU.add
             )
-            z_of[n] = z
             exp_m1_of[n] = exp_m1
 
         def finish_and_store(n):
-            b, j = divmod(n, PAIRS)
+            b, first = banks[n]
             elu = work.tile([P, PAIR, PIX], F32, name="elu")
             nc.vector.scalar_tensor_tensor(
                 out=elu[:], in0=exp_m1_of[n][:], scalar=0.0, in1=z_of[n][:], op0=ALU.min, op1=ALU.max
             )
-            nc.sync.dma_start(out=out_banks[b, j], in_=elu[:])
+            nc.sync.dma_start(out=out_tiles[b, :, first : first + PAIR, :], in_=elu[:])
 
-        passes_and_exp(0)
+        for pix0 in (0, HALF_PIX):
+            for n in range(PAIRS):
+                passes(n, pix0, HALF_PIX)
+        for n in range(PAIRS, B * PAIRS):
+            passes(n, 0, PIX)
+        exp_minus_one(0)
         for n in range(1, B * PAIRS):
-            passes_and_exp(n)
+            exp_minus_one(n)
             finish_and_store(n - 1)
         finish_and_store(B * PAIRS - 1)

@@ -1,6 +1,7 @@
 from contextlib import ExitStack
 
 import concourse.mybir as mybir
+from concourse.masks import make_identity
 
 F32 = mybir.dt.float32
 BF16 = mybir.dt.bfloat16
@@ -30,8 +31,6 @@ BANKS = 8
 
 SCALAR_SHARE_OF_8 = 3
 
-VECTOR_MINUS_ONE = (0, 4)
-
 FLOPS = 2 * B * PIX * C * REP * HID
 
 
@@ -39,91 +38,88 @@ def tile_qca_operator_deep_pa_s_kernel(tc, x_cat, w1_words, w1_scales, out):
     nc = tc.nc
     with ExitStack() as ctx:
         keep = ctx.enter_context(tc.tile_pool(name="keep", bufs=1))
-        work = ctx.enter_context(tc.tile_pool(name="work", bufs=B * PAIRS))
+        work = ctx.enter_context(tc.tile_pool(name="work", bufs=B * PAIRS + 1))
         psum = ctx.enter_context(tc.psum_pool(name="psum", bufs=BANKS))
-
-        x_by_channel = x_cat.rearrange("b c h w -> c b h w")
-
-        x_updown = keep.tile([P, B, H, W], BF16)
-        nc.sync.dma_start(out=x_updown[0:C, :, 1:H, :], in_=x_by_channel[:, :, 0 : H - 1, :])
-        nc.sync.dma_start(out=x_updown[C:P, :, 0 : H - 1, :], in_=x_by_channel[:, :, 1:H, :])
-        nc.vector.memset(x_updown[0:C, :, 0:1, :], 0.0)
-        nc.vector.memset(x_updown[C:P, :, H - 1 : H, :], 0.0)
-
-        x_twice = keep.tile([P, B, H, W], BF16)
-        for copy in range(COPIES):
-            nc.sync.dma_start(out=x_twice[copy:P:COPIES], in_=x_by_channel)
-
-        w_words = keep.tile([P, HID * FP4_WORD_BYTES], U8, align_bytes=64)
-        nc.sync.dma_start(out=w_words[:].bitcast(I32), in_=w1_words[0].bitcast(I32))
-
-        w_scales = keep.tile([P, HID], U8, align_bytes=64)
-        nc.vector.memset(w_scales[:].bitcast(I32), 0)
-        for quadrant in range(4):
-            nc.sync.dma_start(
-                out=w_scales[32 * quadrant : 32 * quadrant + 4, :].bitcast(I32),
-                in_=w1_scales[0, 4 * quadrant : 4 * quadrant + 4, :].bitcast(I32),
-            )
-
-        warm = keep.tile([P, 1], F32)
-        nc.vector.memset(warm[:], 0.0)
-        nc.scalar.activation(out=warm[:], in_=warm[:], func=ACT.Exp)
-
-        pick = keep.tile([P, P], BF16)
-        nc.gpsimd.memset(pick[:], 0.0)
-        for half in range(2):
-            nc.gpsimd.affine_select(
-                out=pick[:],
-                in_=pick[:],
-                compare_op=ALU.not_equal,
-                fill=1.0,
-                base=-C * half,
-                pattern=[[-1, C], [0, COPIES]],
-                channel_multiplier=1,
-            )
-        pick_cols = pick[:]
-
-        sides = keep.tile([P, B, H, W], F32)
-        for b in range(B):
-            nc.vector.tensor_tensor(
-                out=sides[:, b, :, 1 : W - 1], in0=x_twice[:, b, :, 0 : W - 2], in1=x_twice[:, b, :, 2:W], op=ALU.add
-            )
-        nc.scalar.copy(out=sides[:, :, :, 0 : W : W - 1], in_=x_twice[:, :, :, 1 : W - 1 : W - 3])
-
-        nbr = keep.tile([P, B, H, W], BF16)
-        nbr_pix = nbr[:].rearrange("p b h w -> p b (h w)")
-        xn4 = keep.tile([P, B, PIX, PACK], BF16, align_bytes=64)
-        x_words = keep.tile([P, B, PIX], U32, align_bytes=64)
-        x_scales = keep.tile([P, B, PIX], U8, align_bytes=64)
-
-        def neighbour_sum(b, row0, rows):
-            part = x_updown[:, b, row0 : row0 + rows, :]
-            six = psum.tile([P, rows, W], F32, name="six", tag="bank")
-            nc.tensor.matmul(out=six[:], lhsT=pick_cols, rhs=part, start=True, stop=False)
-            nc.tensor.matmul(out=six[:, :, 1:W], lhsT=pick_cols, rhs=part[:, :, 0 : W - 1], start=False, stop=False)
-            nc.tensor.matmul(out=six[:, :, 0 : W - 1], lhsT=pick_cols, rhs=part[:, :, 1:W], start=False, stop=True)
-            nc.vector.tensor_tensor(
-                out=nbr[:, b, row0 : row0 + rows, :], in0=six[:], in1=sides[:, b, row0 : row0 + rows, :], op=ALU.add
-            )
-
-        def repeat(b, pix0, pixels):
-            cut = pix0 + pixels * SCALAR_SHARE_OF_8 // 8
-            nc.scalar.copy(
-                out=xn4[:, b, pix0:cut, :], in_=nbr_pix[:, b, pix0:cut].unsqueeze(2).to_broadcast([P, cut - pix0, PACK])
-            )
-            nc.vector.tensor_copy(
-                out=xn4[:, b, cut : pix0 + pixels, :],
-                in_=nbr_pix[:, b, cut : pix0 + pixels].unsqueeze(2).to_broadcast([P, pix0 + pixels - cut, PACK]),
-            )
-
-        def quantise(b, pix0, pixels):
-            nc.vector.quantize_mx(
-                out=x_words[:, b, pix0 : pix0 + pixels].bitcast(FP8X4),
-                scales=x_scales[:, b, pix0 : pix0 + pixels],
-                in_=xn4[:, b, pix0 : pix0 + pixels, :].rearrange("p w t -> p (w t)"),
-            )
-
         with tc.manual_schedule(engines={mybir.EngineType.DVE}):
+
+            x_by_channel = x_cat.rearrange("b c h w -> c b h w")
+
+            x_updown = keep.tile([P, B, H, W], BF16)
+            nc.sync.dma_start(out=x_updown[0:C, :, 1:H, :], in_=x_by_channel[:, :, 0 : H - 1, :])
+            nc.sync.dma_start(out=x_updown[C:P, :, 0 : H - 1, :], in_=x_by_channel[:, :, 1:H, :])
+            nc.vector.memset(x_updown[0:C, :, 0:1, :], 0.0)
+            nc.vector.memset(x_updown[C:P, :, H - 1 : H, :], 0.0)
+
+            x_twice = keep.tile([P, B, H, W], BF16)
+            for copy in range(COPIES):
+                nc.sync.dma_start(out=x_twice[copy:P:COPIES], in_=x_by_channel)
+
+            w_words = keep.tile([P, HID * FP4_WORD_BYTES], U8, align_bytes=64)
+            nc.sync.dma_start(out=w_words[:].bitcast(I32), in_=w1_words[0].bitcast(I32))
+
+            w_scales = keep.tile([P, HID], U8, align_bytes=64)
+            nc.vector.memset(w_scales[:].bitcast(I32), 0)
+            for quadrant in range(4):
+                nc.sync.dma_start(
+                    out=w_scales[32 * quadrant : 32 * quadrant + 4, :].bitcast(I32),
+                    in_=w1_scales[0, 4 * quadrant : 4 * quadrant + 4, :].bitcast(I32),
+                )
+
+            warm = keep.tile([P, 1], F32)
+            nc.vector.memset(warm[:], 0.0)
+            nc.scalar.activation(out=warm[:], in_=warm[:], func=ACT.Exp)
+
+            ident = keep.tile([P, P], BF16)
+            make_identity(nc, ident[:])
+            pick = keep.tile([P, C, COPIES], BF16)
+            nc.vector.tensor_tensor(
+                out=pick[:],
+                in0=ident[:, 0:C].unsqueeze(2).to_broadcast([P, C, COPIES]),
+                in1=ident[:, C:P].unsqueeze(2).to_broadcast([P, C, COPIES]),
+                op=ALU.add,
+            )
+            pick_cols = pick[:].rearrange("k c d -> k (c d)")
+
+            sides = keep.tile([P, B, H, W], F32)
+            for b in range(B):
+                nc.vector.tensor_tensor(
+                    out=sides[:, b, :, 1 : W - 1], in0=x_twice[:, b, :, 0 : W - 2], in1=x_twice[:, b, :, 2:W], op=ALU.add
+                )
+            nc.scalar.copy(out=sides[:, :, :, 0 : W : W - 1], in_=x_twice[:, :, :, 1 : W - 1 : W - 3])
+
+            nbr = keep.tile([P, B, H, W], BF16)
+            nbr_pix = nbr[:].rearrange("p b h w -> p b (h w)")
+            xn4 = keep.tile([P, B, PIX, PACK], BF16, align_bytes=64)
+            x_words = keep.tile([P, B, PIX], U32, align_bytes=64)
+            x_scales = keep.tile([P, B, PIX], U8, align_bytes=64)
+
+            def neighbour_sum(b, row0, rows):
+                part = x_updown[:, b, row0 : row0 + rows, :]
+                six = psum.tile([P, rows, W], F32, name="six", tag="bank")
+                nc.tensor.matmul(out=six[:], lhsT=pick_cols, rhs=part, start=True, stop=False)
+                nc.tensor.matmul(out=six[:, :, 1:W], lhsT=pick_cols, rhs=part[:, :, 0 : W - 1], start=False, stop=False)
+                nc.tensor.matmul(out=six[:, :, 0 : W - 1], lhsT=pick_cols, rhs=part[:, :, 1:W], start=False, stop=True)
+                nc.vector.tensor_tensor(
+                    out=nbr[:, b, row0 : row0 + rows, :], in0=six[:], in1=sides[:, b, row0 : row0 + rows, :], op=ALU.add
+                )
+
+            def repeat(b, pix0, pixels):
+                cut = pix0 + pixels * SCALAR_SHARE_OF_8 // 8
+                nc.scalar.copy(
+                    out=xn4[:, b, pix0:cut, :], in_=nbr_pix[:, b, pix0:cut].unsqueeze(2).to_broadcast([P, cut - pix0, PACK])
+                )
+                nc.vector.tensor_copy(
+                    out=xn4[:, b, cut : pix0 + pixels, :],
+                    in_=nbr_pix[:, b, cut : pix0 + pixels].unsqueeze(2).to_broadcast([P, pix0 + pixels - cut, PACK]),
+                )
+
+            def quantise(b, pix0, pixels):
+                nc.vector.quantize_mx(
+                    out=x_words[:, b, pix0 : pix0 + pixels].bitcast(FP8X4),
+                    scales=x_scales[:, b, pix0 : pix0 + pixels],
+                    in_=xn4[:, b, pix0 : pix0 + pixels, :].rearrange("p w t -> p (w t)"),
+                )
+
             neighbour_sum(0, 0, HALF_ROWS)
             repeat(0, 0, HALF_PIX)
             neighbour_sum(0, HALF_ROWS, HALF_ROWS)
@@ -134,16 +130,18 @@ def tile_qca_operator_deep_pa_s_kernel(tc, x_cat, w1_words, w1_scales, out):
             repeat(1, 0, PIX)
             quantise(1, 0, PIX)
 
-        banks = [(b, m) for b in range(B) for m in range(0, TILES, PAIR)]
+        units = [(0, 0, 1), (0, 1, 1)] + [(0, m, PAIR) for m in range(PAIR, TILES, PAIR)]
+        first_of_batch_1 = len(units)
+        units += [(1, m, PAIR) for m in range(0, TILES, PAIR)]
         out_tiles = out.rearrange("b (m p) h w -> b p m (h w)", p=P)
         z_of = {}
         exp_m1_of = {}
 
         def passes(n, pix0, pixels):
-            b, first = banks[n]
+            b, first, count = units[n]
             if n not in z_of:
-                z_of[n] = psum.tile([P, PAIR, PIX], F32, name="z", tag="bank")
-            for i in range(PAIR):
+                z_of[n] = psum.tile([P, count, PIX], F32, name="z", tag="bank")
+            for i in range(count):
                 m = first + i
                 nc.tensor.matmul_mx(
                     out=z_of[n][:, i, pix0 : pix0 + pixels],
@@ -156,30 +154,45 @@ def tile_qca_operator_deep_pa_s_kernel(tc, x_cat, w1_words, w1_scales, out):
                 )
 
         def exp_minus_one(n):
-            exp_z = work.tile([P, PAIR, PIX], F32, name="exp_z")
+            count = units[n][2]
+            exp_z = work.tile([P, count, PIX], F32, name="exp_z")
             nc.scalar.activation(out=exp_z[:], in_=z_of[n][:], func=ACT.Exp)
-            exp_m1 = work.tile([P, PAIR, PIX], F32, name="exp_m1")
-            minus_one_engine = nc.vector if n in VECTOR_MINUS_ONE else nc.gpsimd
-            minus_one_engine.tensor_scalar(
-                out=exp_m1[:], in0=exp_z[:], scalar1=1.0, scalar2=-1.0, op0=ALU.mult, op1=ALU.add
-            )
+            if n == 0:
+                relu_z = work.tile([P, count, PIX], F32, name="relu_z")
+                nc.vector.tensor_scalar(out=relu_z[:], in0=z_of[n][:], scalar1=0.0, scalar2=None, op0=ALU.max)
+                exp_m1_of[n] = (exp_z, relu_z)
+                return
+            exp_m1 = work.tile([P, count, PIX], F32, name="exp_m1")
+            if n == len(units) - 1:
+                nc.scalar.activation(out=exp_m1[:], in_=exp_z[:], func=ACT.Copy, bias=-1.0)
+            else:
+                minus_one_engine = nc.vector if n == first_of_batch_1 else nc.gpsimd
+                minus_one_engine.tensor_scalar(
+                    out=exp_m1[:], in0=exp_z[:], scalar1=1.0, scalar2=-1.0, op0=ALU.mult, op1=ALU.add
+                )
             exp_m1_of[n] = exp_m1
 
         def finish_and_store(n):
-            b, first = banks[n]
-            elu = work.tile([P, PAIR, PIX], F32, name="elu")
-            nc.vector.scalar_tensor_tensor(
-                out=elu[:], in0=exp_m1_of[n][:], scalar=0.0, in1=z_of[n][:], op0=ALU.min, op1=ALU.max
-            )
-            nc.sync.dma_start(out=out_tiles[b, :, first : first + PAIR, :], in_=elu[:])
+            b, first, count = units[n]
+            elu = work.tile([P, count, PIX], F32, name="elu")
+            if n == 0:
+                exp_z, relu_z = exp_m1_of[n]
+                nc.vector.scalar_tensor_tensor(
+                    out=elu[:], in0=exp_z[:], scalar=-1.0, in1=relu_z[:], op0=ALU.add, op1=ALU.min
+                )
+            else:
+                nc.vector.scalar_tensor_tensor(
+                    out=elu[:], in0=exp_m1_of[n][:], scalar=0.0, in1=z_of[n][:], op0=ALU.min, op1=ALU.max
+                )
+            nc.sync.dma_start(out=out_tiles[b, :, first : first + count, :], in_=elu[:])
 
         for pix0 in (0, HALF_PIX):
-            for n in range(PAIRS):
+            for n in range(first_of_batch_1):
                 passes(n, pix0, HALF_PIX)
-        for n in range(PAIRS, B * PAIRS):
+        for n in range(first_of_batch_1, len(units)):
             passes(n, 0, PIX)
         exp_minus_one(0)
-        for n in range(1, B * PAIRS):
+        for n in range(1, len(units)):
             exp_minus_one(n)
             finish_and_store(n - 1)
-        finish_and_store(B * PAIRS - 1)
+        finish_and_store(len(units) - 1)

@@ -31,6 +31,8 @@ BANKS = 8
 
 SCALAR_SHARE_OF_8 = 3
 
+EARLY_TILES = 3
+
 FLOPS = 2 * B * PIX * C * REP * HID
 
 
@@ -40,7 +42,7 @@ def tile_qca_operator_deep_pa_s_kernel(tc, x_cat, w1_words, w1_scales, out):
         keep = ctx.enter_context(tc.tile_pool(name="keep", bufs=1))
         work = ctx.enter_context(tc.tile_pool(name="work", bufs=B * PAIRS + 1))
         psum = ctx.enter_context(tc.psum_pool(name="psum", bufs=BANKS))
-        with tc.manual_schedule(engines={mybir.EngineType.DVE}):
+        with tc.manual_schedule(engines={mybir.EngineType.DVE, mybir.EngineType.PE}):
 
             x_by_channel = x_cat.rearrange("b c h w -> c b h w")
 
@@ -120,29 +122,16 @@ def tile_qca_operator_deep_pa_s_kernel(tc, x_cat, w1_words, w1_scales, out):
                     in_=xn4[:, b, pix0 : pix0 + pixels, :].rearrange("p w t -> p (w t)"),
                 )
 
-            neighbour_sum(0, 0, HALF_ROWS)
-            repeat(0, 0, HALF_PIX)
-            neighbour_sum(0, HALF_ROWS, HALF_ROWS)
-            quantise(0, 0, HALF_PIX)
-            repeat(0, HALF_PIX, HALF_PIX)
-            neighbour_sum(1, 0, H)
-            quantise(0, HALF_PIX, HALF_PIX)
-            repeat(1, 0, PIX)
-            quantise(1, 0, PIX)
+            units = [(0, 0, 1), (0, 1, 1)] + [(0, m, PAIR) for m in range(PAIR, TILES, PAIR)]
+            first_of_batch_1 = len(units)
+            units += [(1, m, PAIR) for m in range(0, TILES, PAIR)]
+            unit_of_tile = {(b, first + i): (n, i) for n, (b, first, count) in enumerate(units) for i in range(count)}
+            z_of = {}
 
-        units = [(0, 0, 1), (0, 1, 1)] + [(0, m, PAIR) for m in range(PAIR, TILES, PAIR)]
-        first_of_batch_1 = len(units)
-        units += [(1, m, PAIR) for m in range(0, TILES, PAIR)]
-        out_tiles = out.rearrange("b (m p) h w -> b p m (h w)", p=P)
-        z_of = {}
-        exp_m1_of = {}
-
-        def passes(n, pix0, pixels):
-            b, first, count = units[n]
-            if n not in z_of:
-                z_of[n] = psum.tile([P, count, PIX], F32, name="z", tag="bank")
-            for i in range(count):
-                m = first + i
+            def one_pass(b, m, pix0, pixels):
+                n, i = unit_of_tile[(b, m)]
+                if n not in z_of:
+                    z_of[n] = psum.tile([P, units[n][2], PIX], F32, name="z", tag="bank")
                 nc.tensor.matmul_mx(
                     out=z_of[n][:, i, pix0 : pix0 + pixels],
                     lhsT=w_words[:, m * P * FP4_WORD_BYTES : (m + 1) * P * FP4_WORD_BYTES].bitcast(FP4X4),
@@ -152,6 +141,28 @@ def tile_qca_operator_deep_pa_s_kernel(tc, x_cat, w1_words, w1_scales, out):
                     start=True,
                     stop=True,
                 )
+
+            neighbour_sum(0, 0, HALF_ROWS)
+            repeat(0, 0, HALF_PIX)
+            neighbour_sum(0, HALF_ROWS, HALF_ROWS)
+            quantise(0, 0, HALF_PIX)
+            repeat(0, HALF_PIX, HALF_PIX)
+            neighbour_sum(1, 0, H)
+            for m in range(EARLY_TILES):
+                one_pass(0, m, 0, HALF_PIX)
+            quantise(0, HALF_PIX, HALF_PIX)
+            for m in range(EARLY_TILES):
+                one_pass(0, m, HALF_PIX, HALF_PIX)
+            for m in range(EARLY_TILES, TILES):
+                one_pass(0, m, 0, HALF_PIX)
+                one_pass(0, m, HALF_PIX, HALF_PIX)
+            repeat(1, 0, PIX)
+            quantise(1, 0, PIX)
+            for m in range(TILES):
+                one_pass(1, m, 0, PIX)
+
+        out_tiles = out.rearrange("b (m p) h w -> b p m (h w)", p=P)
+        exp_m1_of = {}
 
         def exp_minus_one(n):
             count = units[n][2]
@@ -186,11 +197,6 @@ def tile_qca_operator_deep_pa_s_kernel(tc, x_cat, w1_words, w1_scales, out):
                 )
             nc.sync.dma_start(out=out_tiles[b, :, first : first + count, :], in_=elu[:])
 
-        for pix0 in (0, HALF_PIX):
-            for n in range(first_of_batch_1):
-                passes(n, pix0, HALF_PIX)
-        for n in range(first_of_batch_1, len(units)):
-            passes(n, 0, PIX)
         exp_minus_one(0)
         for n in range(1, len(units)):
             exp_minus_one(n)

@@ -191,11 +191,19 @@ def tile_qca_operator_deep_pa_s_kernel(tc, x_cat, w1_words, w1_scales, out):
                 nc.vector.scalar_tensor_tensor(
                     out=elu[:], in0=exp_z[:], scalar=-1.0, in1=relu_z[:], op0=ALU.add, op1=ALU.min
                 )
-            else:
+                nc.sync.dma_start(out=out_tiles[b, :, first : first + count, :], in_=elu[:])
+                return
+            step = 1 if n == len(units) - 1 else count
+            for i in range(0, count, step):
                 nc.vector.scalar_tensor_tensor(
-                    out=elu[:], in0=exp_m1_of[n][:], scalar=0.0, in1=z_of[n][:], op0=ALU.min, op1=ALU.max
+                    out=elu[:, i : i + step, :],
+                    in0=exp_m1_of[n][:, i : i + step, :],
+                    scalar=0.0,
+                    in1=z_of[n][:, i : i + step, :],
+                    op0=ALU.min,
+                    op1=ALU.max,
                 )
-            nc.sync.dma_start(out=out_tiles[b, :, first : first + count, :], in_=elu[:])
+                nc.sync.dma_start(out=out_tiles[b, :, first + i : first + i + step, :], in_=elu[:, i : i + step, :])
 
         exp_minus_one(0)
         for n in range(1, len(units)):

@@ -29,9 +29,10 @@ HALF_ROWS = H // 2
 HALF_PIX = PIX // 2
 BANKS = 8
 
-SCALAR_SHARE_OF_8 = 3
+SCALAR_PIX = HALF_PIX * 3 // 8
+GPSIMD_PIX = PIX * 3 // 8
 
-EARLY_TILES = 3
+SPLIT_TILES = 4
 
 FLOPS = 2 * B * PIX * C * REP * HID
 
@@ -40,9 +41,11 @@ def tile_qca_operator_deep_pa_s_kernel(tc, x_cat, w1_words, w1_scales, out):
     nc = tc.nc
     with ExitStack() as ctx:
         keep = ctx.enter_context(tc.tile_pool(name="keep", bufs=1))
-        work = ctx.enter_context(tc.tile_pool(name="work", bufs=B * PAIRS + 1))
+        work = ctx.enter_context(tc.tile_pool(name="work", bufs=B * PAIRS + 2))
         psum = ctx.enter_context(tc.psum_pool(name="psum", bufs=BANKS))
-        with tc.manual_schedule(engines={mybir.EngineType.DVE, mybir.EngineType.PE}):
+        with tc.manual_schedule(
+            engines={mybir.EngineType.DVE, mybir.EngineType.PE, mybir.EngineType.Activation, mybir.EngineType.Pool}
+        ):
 
             x_by_channel = x_cat.rearrange("b c h w -> c b h w")
 
@@ -89,30 +92,53 @@ def tile_qca_operator_deep_pa_s_kernel(tc, x_cat, w1_words, w1_scales, out):
                 )
             nc.scalar.copy(out=sides[:, :, :, 0 : W : W - 1], in_=x_twice[:, :, :, 1 : W - 1 : W - 3])
 
-            nbr = keep.tile([P, B, H, W], BF16)
-            nbr_pix = nbr[:].rearrange("p b h w -> p b (h w)")
+            sides_pix = sides[:].rearrange("p b h w -> p b (h w)")
+            nbr = keep.tile([P, B, PIX], BF16)
             xn4 = keep.tile([P, B, PIX, PACK], BF16, align_bytes=64)
             x_words = keep.tile([P, B, PIX], U32, align_bytes=64)
             x_scales = keep.tile([P, B, PIX], U8, align_bytes=64)
 
-            def neighbour_sum(b, row0, rows):
+            six_of = {}
+
+            def six_neighbours(b, row0, rows):
                 part = x_updown[:, b, row0 : row0 + rows, :]
                 six = psum.tile([P, rows, W], F32, name="six", tag="bank")
                 nc.tensor.matmul(out=six[:], lhsT=pick_cols, rhs=part, start=True, stop=False)
                 nc.tensor.matmul(out=six[:, :, 1:W], lhsT=pick_cols, rhs=part[:, :, 0 : W - 1], start=False, stop=False)
                 nc.tensor.matmul(out=six[:, :, 0 : W - 1], lhsT=pick_cols, rhs=part[:, :, 1:W], start=False, stop=True)
+                six_of[(b, row0 * W)] = six[:].rearrange("p h w -> p (h w)")
+
+            def add_once(b, pix0, count):
                 nc.vector.tensor_tensor(
-                    out=nbr[:, b, row0 : row0 + rows, :], in0=six[:], in1=sides[:, b, row0 : row0 + rows, :], op=ALU.add
+                    out=nbr[:, b, pix0 : pix0 + count],
+                    in0=six_of[(b, pix0)][:, 0:count],
+                    in1=sides_pix[:, b, pix0 : pix0 + count],
+                    op=ALU.add,
                 )
 
-            def repeat(b, pix0, pixels):
-                cut = pix0 + pixels * SCALAR_SHARE_OF_8 // 8
+            def repeat_on_scalar(b, pix0, count):
                 nc.scalar.copy(
-                    out=xn4[:, b, pix0:cut, :], in_=nbr_pix[:, b, pix0:cut].unsqueeze(2).to_broadcast([P, cut - pix0, PACK])
+                    out=xn4[:, b, pix0 : pix0 + count, :],
+                    in_=nbr[:, b, pix0 : pix0 + count].unsqueeze(2).to_broadcast([P, count, PACK]),
                 )
-                nc.vector.tensor_copy(
-                    out=xn4[:, b, cut : pix0 + pixels, :],
-                    in_=nbr_pix[:, b, cut : pix0 + pixels].unsqueeze(2).to_broadcast([P, pix0 + pixels - cut, PACK]),
+
+            def repeat_on_gpsimd(b, pix0, count):
+                nc.gpsimd.tensor_scalar(
+                    out=xn4[:, b, pix0 : pix0 + count, :],
+                    in0=nbr[:, b, pix0 : pix0 + count].unsqueeze(2).to_broadcast([P, count, PACK]),
+                    scalar1=1.0,
+                    scalar2=0.0,
+                    op0=ALU.mult,
+                    op1=ALU.add,
+                )
+
+            def add_four_times(b, pix0, skip, pixels):
+                shape = [P, pixels - skip, PACK]
+                nc.vector.tensor_tensor(
+                    out=xn4[:, b, pix0 + skip : pix0 + pixels, :],
+                    in0=six_of[(b, pix0)][:, skip:pixels].unsqueeze(2).to_broadcast(shape),
+                    in1=sides_pix[:, b, pix0 + skip : pix0 + pixels].unsqueeze(2).to_broadcast(shape),
+                    op=ALU.add,
                 )
 
             def quantise(b, pix0, pixels):
@@ -122,91 +148,97 @@ def tile_qca_operator_deep_pa_s_kernel(tc, x_cat, w1_words, w1_scales, out):
                     in_=xn4[:, b, pix0 : pix0 + pixels, :].rearrange("p w t -> p (w t)"),
                 )
 
-            units = [(0, 0, 1), (0, 1, 1)] + [(0, m, PAIR) for m in range(PAIR, TILES, PAIR)]
+            units = [(0, 0, PAIR, 0, HALF_PIX), (0, PAIR, PAIR, 0, HALF_PIX), (0, 0, SPLIT_TILES, HALF_PIX, HALF_PIX)]
+            units += [(0, m, PAIR, 0, PIX) for m in range(SPLIT_TILES, TILES, PAIR)]
             first_of_batch_1 = len(units)
-            units += [(1, m, PAIR) for m in range(0, TILES, PAIR)]
-            unit_of_tile = {(b, first + i): (n, i) for n, (b, first, count) in enumerate(units) for i in range(count)}
+            units += [(1, m, PAIR, 0, PIX) for m in range(0, TILES, PAIR)]
             z_of = {}
 
-            def one_pass(b, m, pix0, pixels):
-                n, i = unit_of_tile[(b, m)]
-                if n not in z_of:
-                    z_of[n] = psum.tile([P, units[n][2], PIX], F32, name="z", tag="bank")
-                nc.tensor.matmul_mx(
-                    out=z_of[n][:, i, pix0 : pix0 + pixels],
-                    lhsT=w_words[:, m * P * FP4_WORD_BYTES : (m + 1) * P * FP4_WORD_BYTES].bitcast(FP4X4),
-                    lhsT_scale=w_scales[:, m * P : (m + 1) * P],
-                    rhs=x_words[:, b, pix0 : pix0 + pixels].bitcast(FP8X4),
-                    rhs_scale=x_scales[:, b, pix0 : pix0 + pixels],
-                    start=True,
-                    stop=True,
-                )
+            def multiply(n):
+                b, first, count, pix0, pixels = units[n]
+                z_of[n] = psum.tile([P, count, pixels], F32, name="z", tag="bank")
+                for i in range(count):
+                    m = first + i
+                    nc.tensor.matmul_mx(
+                        out=z_of[n][:, i, :],
+                        lhsT=w_words[:, m * P * FP4_WORD_BYTES : (m + 1) * P * FP4_WORD_BYTES].bitcast(FP4X4),
+                        lhsT_scale=w_scales[:, m * P : (m + 1) * P],
+                        rhs=x_words[:, b, pix0 : pix0 + pixels].bitcast(FP8X4),
+                        rhs_scale=x_scales[:, b, pix0 : pix0 + pixels],
+                        start=True,
+                        stop=True,
+                    )
 
-            neighbour_sum(0, 0, HALF_ROWS)
-            repeat(0, 0, HALF_PIX)
-            neighbour_sum(0, HALF_ROWS, HALF_ROWS)
+            out_tiles = out.rearrange("b (m p) h w -> b p m (h w)", p=P)
+            exp_of, exp_m1_of = {}, {}
+
+            def exponential(n):
+                b, first, count, pix0, pixels = units[n]
+                exp_of[n] = work.tile([P, count, pixels], F32, name="exp_z")
+                nc.scalar.activation(out=exp_of[n][:], in_=z_of[n][:], func=ACT.Exp)
+
+            def subtract(engine, n):
+                b, first, count, pix0, pixels = units[n]
+                exp_m1_of[n] = work.tile([P, count, pixels], F32, name="exp_m1")
+                if engine == nc.scalar:
+                    nc.scalar.activation(out=exp_m1_of[n][:], in_=exp_of[n][:], func=ACT.Copy, bias=-1.0)
+                else:
+                    engine.tensor_scalar(
+                        out=exp_m1_of[n][:], in0=exp_of[n][:], scalar1=1.0, scalar2=-1.0, op0=ALU.mult, op1=ALU.add
+                    )
+
+            def finish_and_store(n):
+                b, first, count, pix0, pixels = units[n]
+                elu = work.tile([P, count, pixels], F32, name="elu")
+                step = 1 if n == len(units) - 1 else count
+                for i in range(0, count, step):
+                    nc.vector.scalar_tensor_tensor(
+                        out=elu[:, i : i + step, :],
+                        in0=exp_m1_of[n][:, i : i + step, :],
+                        scalar=0.0,
+                        in1=z_of[n][:, i : i + step, :],
+                        op0=ALU.min,
+                        op1=ALU.max,
+                    )
+                    nc.sync.dma_start(
+                        out=out_tiles[b, :, first + i : first + i + step, pix0 : pix0 + pixels], in_=elu[:, i : i + step, :]
+                    )
+
+            six_neighbours(0, 0, HALF_ROWS)
+            add_once(0, 0, SCALAR_PIX)
+            repeat_on_scalar(0, 0, SCALAR_PIX)
+            add_four_times(0, 0, SCALAR_PIX, HALF_PIX)
+            six_neighbours(0, HALF_ROWS, HALF_ROWS)
+            add_once(0, HALF_PIX, SCALAR_PIX)
+            repeat_on_scalar(0, HALF_PIX, SCALAR_PIX)
+            add_four_times(0, HALF_PIX, SCALAR_PIX, HALF_PIX)
+            six_neighbours(1, 0, H)
             quantise(0, 0, HALF_PIX)
-            repeat(0, HALF_PIX, HALF_PIX)
-            neighbour_sum(1, 0, H)
-            for m in range(EARLY_TILES):
-                one_pass(0, m, 0, HALF_PIX)
+            for n in (0, 1):
+                multiply(n)
+                exponential(n)
+            add_once(1, 0, GPSIMD_PIX)
+            repeat_on_gpsimd(1, 0, GPSIMD_PIX)
             quantise(0, HALF_PIX, HALF_PIX)
-            for m in range(EARLY_TILES):
-                one_pass(0, m, HALF_PIX, HALF_PIX)
-            for m in range(EARLY_TILES, TILES):
-                one_pass(0, m, 0, HALF_PIX)
-                one_pass(0, m, HALF_PIX, HALF_PIX)
-            repeat(1, 0, PIX)
+            for n in range(2, first_of_batch_1):
+                multiply(n)
+            add_four_times(1, 0, GPSIMD_PIX, PIX)
+            subtract(nc.vector, 0)
             quantise(1, 0, PIX)
-            for m in range(TILES):
-                one_pass(1, m, 0, PIX)
-
-        out_tiles = out.rearrange("b (m p) h w -> b p m (h w)", p=P)
-        exp_m1_of = {}
-
-        def exp_minus_one(n):
-            count = units[n][2]
-            exp_z = work.tile([P, count, PIX], F32, name="exp_z")
-            nc.scalar.activation(out=exp_z[:], in_=z_of[n][:], func=ACT.Exp)
-            if n == 0:
-                relu_z = work.tile([P, count, PIX], F32, name="relu_z")
-                nc.vector.tensor_scalar(out=relu_z[:], in0=z_of[n][:], scalar1=0.0, scalar2=None, op0=ALU.max)
-                exp_m1_of[n] = (exp_z, relu_z)
-                return
-            exp_m1 = work.tile([P, count, PIX], F32, name="exp_m1")
-            if n == len(units) - 1:
-                nc.scalar.activation(out=exp_m1[:], in_=exp_z[:], func=ACT.Copy, bias=-1.0)
-            else:
-                minus_one_engine = nc.vector if n == first_of_batch_1 else nc.gpsimd
-                minus_one_engine.tensor_scalar(
-                    out=exp_m1[:], in0=exp_z[:], scalar1=1.0, scalar2=-1.0, op0=ALU.mult, op1=ALU.add
-                )
-            exp_m1_of[n] = exp_m1
-
-        def finish_and_store(n):
-            b, first, count = units[n]
-            elu = work.tile([P, count, PIX], F32, name="elu")
-            if n == 0:
-                exp_z, relu_z = exp_m1_of[n]
-                nc.vector.scalar_tensor_tensor(
-                    out=elu[:], in0=exp_z[:], scalar=-1.0, in1=relu_z[:], op0=ALU.add, op1=ALU.min
-                )
-                nc.sync.dma_start(out=out_tiles[b, :, first : first + count, :], in_=elu[:])
-                return
-            step = 1 if n == len(units) - 1 else count
-            for i in range(0, count, step):
-                nc.vector.scalar_tensor_tensor(
-                    out=elu[:, i : i + step, :],
-                    in0=exp_m1_of[n][:, i : i + step, :],
-                    scalar=0.0,
-                    in1=z_of[n][:, i : i + step, :],
-                    op0=ALU.min,
-                    op1=ALU.max,
-                )
-                nc.sync.dma_start(out=out_tiles[b, :, first + i : first + i + step, :], in_=elu[:, i : i + step, :])
-
-        exp_minus_one(0)
-        for n in range(1, len(units)):
-            exp_minus_one(n)
-            finish_and_store(n - 1)
-        finish_and_store(len(units) - 1)
+            for n in range(first_of_batch_1, len(units)):
+                multiply(n)
+            on_vector = (0, 2, first_of_batch_1)
+            subtract(nc.gpsimd, 1)
+            for n in range(len(units)):
+                later = n + 2
+                if later < len(units):
+                    exponential(later)
+                    if later == len(units) - 1:
+                        subtract(nc.scalar, later)
+                    elif later not in on_vector:
+                        subtract(nc.gpsimd, later)
+                if n + 1 == first_of_batch_1:
+                    subtract(nc.vector, first_of_batch_1)
+                finish_and_store(n)
+                if n == 1:
+                    subtract(nc.vector, 2)

@@ -227,18 +227,17 @@ def tile_qca_operator_deep_pa_s_kernel(tc, x_cat, w1_words, w1_scales, out):
             quantise(1, 0, PIX)
             for n in range(first_of_batch_1, len(units)):
                 multiply(n)
-            on_vector = (0, 2, first_of_batch_1)
-            subtract(nc.gpsimd, 1)
+            subtract(nc.vector, 1)
             for n in range(len(units)):
                 later = n + 2
                 if later < len(units):
                     exponential(later)
-                    if later == len(units) - 1:
-                        subtract(nc.scalar, later)
-                    elif later not in on_vector:
+                    if 3 < later < len(units) - 2:
                         subtract(nc.gpsimd, later)
-                if n + 1 == first_of_batch_1:
-                    subtract(nc.vector, first_of_batch_1)
+                if later == len(units) - 1:
+                    subtract(nc.scalar, later - 1)
+                    subtract(nc.scalar, later)
                 finish_and_store(n)
                 if n == 1:
                     subtract(nc.vector, 2)
+                    subtract(nc.vector, 3)

@@ -30,7 +30,8 @@ HALF_PIX = PIX // 2
 BANKS = 8
 
 SCALAR_PIX = HALF_PIX * 3 // 8
-GPSIMD_PIX = PIX * 3 // 8
+GPSIMD_PIX = 96
+SCALAR_PIX_OF_1 = 48
 
 SPLIT_TILES = 4
 
@@ -50,14 +51,19 @@ def tile_qca_operator_deep_pa_s_kernel(tc, x_cat, w1_words, w1_scales, out):
             x_by_channel = x_cat.rearrange("b c h w -> c b h w")
 
             x_updown = keep.tile([P, B, H, W], BF16)
-            nc.sync.dma_start(out=x_updown[0:C, :, 1:H, :], in_=x_by_channel[:, :, 0 : H - 1, :])
-            nc.sync.dma_start(out=x_updown[C:P, :, 0 : H - 1, :], in_=x_by_channel[:, :, 1:H, :])
+
+            def load_updown(b):
+                nc.sync.dma_start(out=x_updown[0:C, b, 1:H, :], in_=x_by_channel[:, b, 0 : H - 1, :])
+                nc.sync.dma_start(out=x_updown[C:P, b, 0 : H - 1, :], in_=x_by_channel[:, b, 1:H, :])
+
+            load_updown(0)
             nc.vector.memset(x_updown[0:C, :, 0:1, :], 0.0)
             nc.vector.memset(x_updown[C:P, :, H - 1 : H, :], 0.0)
 
             x_twice = keep.tile([P, B, H, W], BF16)
             for copy in range(COPIES):
                 nc.sync.dma_start(out=x_twice[copy:P:COPIES], in_=x_by_channel)
+            load_updown(1)
 
             w_words = keep.tile([P, HID * FP4_WORD_BYTES], U8, align_bytes=64)
             nc.sync.dma_start(out=w_words[:].bitcast(I32), in_=w1_words[0].bitcast(I32))
@@ -214,19 +220,21 @@ def tile_qca_operator_deep_pa_s_kernel(tc, x_cat, w1_words, w1_scales, out):
             add_four_times(0, HALF_PIX, SCALAR_PIX, HALF_PIX)
             six_neighbours(1, 0, H)
             quantise(0, 0, HALF_PIX)
-            for n in (0, 1):
-                multiply(n)
-                exponential(n)
-            add_once(1, 0, GPSIMD_PIX)
+            multiply(0)
+            multiply(1)
+            add_once(1, 0, GPSIMD_PIX + SCALAR_PIX_OF_1)
             repeat_on_gpsimd(1, 0, GPSIMD_PIX)
+            repeat_on_scalar(1, GPSIMD_PIX, SCALAR_PIX_OF_1)
+            exponential(0)
+            exponential(1)
             quantise(0, HALF_PIX, HALF_PIX)
             for n in range(2, first_of_batch_1):
                 multiply(n)
-            add_four_times(1, 0, GPSIMD_PIX, PIX)
-            subtract(nc.vector, 0)
+            add_four_times(1, 0, GPSIMD_PIX + SCALAR_PIX_OF_1, PIX)
             quantise(1, 0, PIX)
             for n in range(first_of_batch_1, len(units)):
                 multiply(n)
+            subtract(nc.vector, 0)
             subtract(nc.vector, 1)
             for n in range(len(units)):
                 later = n + 2

@@ -30,8 +30,7 @@ HALF_PIX = PIX // 2
 BANKS = 8
 
 SCALAR_PIX = HALF_PIX * 3 // 8
-GPSIMD_PIX = 96
-SCALAR_PIX_OF_1 = 48
+SCALAR_PIX_OF_1 = PIX * 5 // 16
 
 SPLIT_TILES = 4
 
@@ -128,16 +127,6 @@ def tile_qca_operator_deep_pa_s_kernel(tc, x_cat, w1_words, w1_scales, out):
                     in_=nbr[:, b, pix0 : pix0 + count].unsqueeze(2).to_broadcast([P, count, PACK]),
                 )
 
-            def repeat_on_gpsimd(b, pix0, count):
-                nc.gpsimd.tensor_scalar(
-                    out=xn4[:, b, pix0 : pix0 + count, :],
-                    in0=nbr[:, b, pix0 : pix0 + count].unsqueeze(2).to_broadcast([P, count, PACK]),
-                    scalar1=1.0,
-                    scalar2=0.0,
-                    op0=ALU.mult,
-                    op1=ALU.add,
-                )
-
             def add_four_times(b, pix0, skip, pixels):
                 shape = [P, pixels - skip, PACK]
                 nc.vector.tensor_tensor(
@@ -222,19 +211,18 @@ def tile_qca_operator_deep_pa_s_kernel(tc, x_cat, w1_words, w1_scales, out):
             quantise(0, 0, HALF_PIX)
             multiply(0)
             multiply(1)
-            add_once(1, 0, GPSIMD_PIX + SCALAR_PIX_OF_1)
-            repeat_on_gpsimd(1, 0, GPSIMD_PIX)
-            repeat_on_scalar(1, GPSIMD_PIX, SCALAR_PIX_OF_1)
+            add_once(1, 0, SCALAR_PIX_OF_1)
+            repeat_on_scalar(1, 0, SCALAR_PIX_OF_1)
             exponential(0)
             exponential(1)
             quantise(0, HALF_PIX, HALF_PIX)
             for n in range(2, first_of_batch_1):
                 multiply(n)
-            add_four_times(1, 0, GPSIMD_PIX + SCALAR_PIX_OF_1, PIX)
+            add_four_times(1, 0, SCALAR_PIX_OF_1, PIX)
+            subtract(nc.vector, 0)
             quantise(1, 0, PIX)
             for n in range(first_of_batch_1, len(units)):
                 multiply(n)
-            subtract(nc.vector, 0)
             subtract(nc.vector, 1)
             for n in range(len(units)):
                 later = n + 2

from contextlib import ExitStack

import concourse.mybir as mybir
from concourse.masks import make_identity

F32 = mybir.dt.float32
BF16 = mybir.dt.bfloat16
I32 = mybir.dt.int32
U32 = mybir.dt.uint32
U8 = mybir.dt.uint8
FP8X4 = mybir.dt.float8_e4m3fn_x4
FP4X4 = mybir.dt.float4_e2m1fn_x4
ALU = mybir.AluOpType
ACT = mybir.ActivationFunctionType

P = 128
PACK = 4
B, C, H, W = 2, 64, 16, 16
REP = 8
HID = 1024
PIX = H * W
COPIES = P // C
FP4_WORD_BYTES = 2
BANK_F32 = 512
PAIR = BANK_F32 // PIX
PAIRS = HID // (P * PAIR)
TILES = HID // P
HALF_ROWS = H // 2
HALF_PIX = PIX // 2
BANKS = 8

SCALAR_PIX = HALF_PIX * 3 // 8
SCALAR_PIX_OF_1 = PIX * 5 // 16

SPLIT_TILES = 4

FLOPS = 2 * B * PIX * C * REP * HID


def tile_qca_operator_deep_pa_s_kernel(tc, x_cat, w1_words, w1_scales, out):
    nc = tc.nc
    with ExitStack() as ctx:
        keep = ctx.enter_context(tc.tile_pool(name="keep", bufs=1))
        work = ctx.enter_context(tc.tile_pool(name="work", bufs=B * PAIRS + 2))
        psum = ctx.enter_context(tc.psum_pool(name="psum", bufs=BANKS))
        with tc.manual_schedule(
            engines={mybir.EngineType.DVE, mybir.EngineType.PE, mybir.EngineType.Activation, mybir.EngineType.Pool}
        ):

            x_by_channel = x_cat.rearrange("b c h w -> c b h w")

            x_updown = keep.tile([P, B, H, W], BF16)

            def load_updown(b):
                nc.sync.dma_start(out=x_updown[0:C, b, 1:H, :], in_=x_by_channel[:, b, 0 : H - 1, :])
                nc.sync.dma_start(out=x_updown[C:P, b, 0 : H - 1, :], in_=x_by_channel[:, b, 1:H, :])

            load_updown(0)
            nc.vector.memset(x_updown[0:C, :, 0:1, :], 0.0)
            nc.vector.memset(x_updown[C:P, :, H - 1 : H, :], 0.0)

            x_twice = keep.tile([P, B, H, W], BF16)
            for copy in range(COPIES):
                nc.sync.dma_start(out=x_twice[copy:P:COPIES], in_=x_by_channel)
            load_updown(1)

            w_words = keep.tile([P, HID * FP4_WORD_BYTES], U8, align_bytes=64)
            nc.sync.dma_start(out=w_words[:].bitcast(I32), in_=w1_words[0].bitcast(I32))

            w_scales = keep.tile([P, HID], U8, align_bytes=64)
            nc.vector.memset(w_scales[:].bitcast(I32), 0)
            for quadrant in range(4):
                nc.sync.dma_start(
                    out=w_scales[32 * quadrant : 32 * quadrant + 4, :].bitcast(I32),
                    in_=w1_scales[0, 4 * quadrant : 4 * quadrant + 4, :].bitcast(I32),
                )

            warm = keep.tile([P, 1], F32)
            nc.vector.memset(warm[:], 0.0)
            nc.scalar.activation(out=warm[:], in_=warm[:], func=ACT.Exp)

            ident = keep.tile([P, P], BF16)
            make_identity(nc, ident[:])
            pick = keep.tile([P, C, COPIES], BF16)
            nc.vector.tensor_tensor(
                out=pick[:],
                in0=ident[:, 0:C].unsqueeze(2).to_broadcast([P, C, COPIES]),
                in1=ident[:, C:P].unsqueeze(2).to_broadcast([P, C, COPIES]),
                op=ALU.add,
            )
            pick_cols = pick[:].rearrange("k c d -> k (c d)")

            sides = keep.tile([P, B, H, W], F32)
            for b in range(B):
                nc.vector.tensor_tensor(
                    out=sides[:, b, :, 1 : W - 1], in0=x_twice[:, b, :, 0 : W - 2], in1=x_twice[:, b, :, 2:W], op=ALU.add
                )
            nc.scalar.copy(out=sides[:, :, :, 0 : W : W - 1], in_=x_twice[:, :, :, 1 : W - 1 : W - 3])

            sides_pix = sides[:].rearrange("p b h w -> p b (h w)")
            nbr = keep.tile([P, B, PIX], BF16)
            xn4 = keep.tile([P, B, PIX, PACK], BF16, align_bytes=64)
            x_words = keep.tile([P, B, PIX], U32, align_bytes=64)
            x_scales = keep.tile([P, B, PIX], U8, align_bytes=64)

            six_of = {}

            def six_neighbours(b, row0, rows):
                part = x_updown[:, b, row0 : row0 + rows, :]
                six = psum.tile([P, rows, W], F32, name="six", tag="bank")
                nc.tensor.matmul(out=six[:], lhsT=pick_cols, rhs=part, start=True, stop=False)
                nc.tensor.matmul(out=six[:, :, 1:W], lhsT=pick_cols, rhs=part[:, :, 0 : W - 1], start=False, stop=False)
                nc.tensor.matmul(out=six[:, :, 0 : W - 1], lhsT=pick_cols, rhs=part[:, :, 1:W], start=False, stop=True)
                six_of[(b, row0 * W)] = six[:].rearrange("p h w -> p (h w)")

            def add_once(b, pix0, count):
                nc.vector.tensor_tensor(
                    out=nbr[:, b, pix0 : pix0 + count],
                    in0=six_of[(b, pix0)][:, 0:count],
                    in1=sides_pix[:, b, pix0 : pix0 + count],
                    op=ALU.add,
                )

            def repeat_on_scalar(b, pix0, count):
                nc.scalar.copy(
                    out=xn4[:, b, pix0 : pix0 + count, :],
                    in_=nbr[:, b, pix0 : pix0 + count].unsqueeze(2).to_broadcast([P, count, PACK]),
                )

            def add_four_times(b, pix0, skip, pixels):
                shape = [P, pixels - skip, PACK]
                nc.vector.tensor_tensor(
                    out=xn4[:, b, pix0 + skip : pix0 + pixels, :],
                    in0=six_of[(b, pix0)][:, skip:pixels].unsqueeze(2).to_broadcast(shape),
                    in1=sides_pix[:, b, pix0 + skip : pix0 + pixels].unsqueeze(2).to_broadcast(shape),
                    op=ALU.add,
                )

            def quantise(b, pix0, pixels):
                nc.vector.quantize_mx(
                    out=x_words[:, b, pix0 : pix0 + pixels].bitcast(FP8X4),
                    scales=x_scales[:, b, pix0 : pix0 + pixels],
                    in_=xn4[:, b, pix0 : pix0 + pixels, :].rearrange("p w t -> p (w t)"),
                )

            units = [(0, 0, PAIR, 0, HALF_PIX), (0, PAIR, PAIR, 0, HALF_PIX), (0, 0, SPLIT_TILES, HALF_PIX, HALF_PIX)]
            units += [(0, m, PAIR, 0, PIX) for m in range(SPLIT_TILES, TILES, PAIR)]
            first_of_batch_1 = len(units)
            units += [(1, m, PAIR, 0, PIX) for m in range(0, TILES, PAIR)]
            z_of = {}

            def multiply(n):
                b, first, count, pix0, pixels = units[n]
                z_of[n] = psum.tile([P, count, pixels], F32, name="z", tag="bank")
                for i in range(count):
                    m = first + i
                    nc.tensor.matmul_mx(
                        out=z_of[n][:, i, :],
                        lhsT=w_words[:, m * P * FP4_WORD_BYTES : (m + 1) * P * FP4_WORD_BYTES].bitcast(FP4X4),
                        lhsT_scale=w_scales[:, m * P : (m + 1) * P],
                        rhs=x_words[:, b, pix0 : pix0 + pixels].bitcast(FP8X4),
                        rhs_scale=x_scales[:, b, pix0 : pix0 + pixels],
                        start=True,
                        stop=True,
                    )

            out_tiles = out.rearrange("b (m p) h w -> b p m (h w)", p=P)
            exp_of, exp_m1_of = {}, {}

            def exponential(n):
                b, first, count, pix0, pixels = units[n]
                exp_of[n] = work.tile([P, count, pixels], F32, name="exp_z")
                nc.scalar.activation(out=exp_of[n][:], in_=z_of[n][:], func=ACT.Exp)

            def subtract(engine, n):
                b, first, count, pix0, pixels = units[n]
                exp_m1_of[n] = work.tile([P, count, pixels], F32, name="exp_m1")
                if engine == nc.scalar:
                    nc.scalar.activation(out=exp_m1_of[n][:], in_=exp_of[n][:], func=ACT.Copy, bias=-1.0)
                else:
                    engine.tensor_scalar(
                        out=exp_m1_of[n][:], in0=exp_of[n][:], scalar1=1.0, scalar2=-1.0, op0=ALU.mult, op1=ALU.add
                    )

            def finish_and_store(n):
                b, first, count, pix0, pixels = units[n]
                elu = work.tile([P, count, pixels], F32, name="elu")
                step = 1 if n == len(units) - 1 else count
                for i in range(0, count, step):
                    nc.vector.scalar_tensor_tensor(
                        out=elu[:, i : i + step, :],
                        in0=exp_m1_of[n][:, i : i + step, :],
                        scalar=0.0,
                        in1=z_of[n][:, i : i + step, :],
                        op0=ALU.min,
                        op1=ALU.max,
                    )
                    nc.sync.dma_start(
                        out=out_tiles[b, :, first + i : first + i + step, pix0 : pix0 + pixels], in_=elu[:, i : i + step, :]
                    )

            six_neighbours(0, 0, HALF_ROWS)
            add_once(0, 0, SCALAR_PIX)
            repeat_on_scalar(0, 0, SCALAR_PIX)
            add_four_times(0, 0, SCALAR_PIX, HALF_PIX)
            six_neighbours(0, HALF_ROWS, HALF_ROWS)
            add_once(0, HALF_PIX, SCALAR_PIX)
            repeat_on_scalar(0, HALF_PIX, SCALAR_PIX)
            add_four_times(0, HALF_PIX, SCALAR_PIX, HALF_PIX)
            six_neighbours(1, 0, H)
            quantise(0, 0, HALF_PIX)
            multiply(0)
            multiply(1)
            add_once(1, 0, SCALAR_PIX_OF_1)
            repeat_on_scalar(1, 0, SCALAR_PIX_OF_1)
            exponential(0)
            exponential(1)
            quantise(0, HALF_PIX, HALF_PIX)
            for n in range(2, first_of_batch_1):
                multiply(n)
            add_four_times(1, 0, SCALAR_PIX_OF_1, PIX)
            subtract(nc.vector, 0)
            quantise(1, 0, PIX)
            for n in range(first_of_batch_1, len(units)):
                multiply(n)
            subtract(nc.vector, 1)
            for n in range(len(units)):
                later = n + 2
                if later < len(units):
                    exponential(later)
                    if 3 < later < len(units) - 2:
                        subtract(nc.gpsimd, later)
                if later == len(units) - 1:
                    subtract(nc.scalar, later - 1)
                    subtract(nc.scalar, later)
                finish_and_store(n)
                if n == 1:
                    subtract(nc.vector, 2)
                    subtract(nc.vector, 3)
